import numpy as np
import ml_dtypes


def mxq(x, axis, fmt="e4m3"):
    dtype, down = {"e4m3": (ml_dtypes.float8_e4m3fn, 7), "e5m2": (ml_dtypes.float8_e5m2, 14)}[fmt]
    v = np.moveaxis(np.asarray(x, np.float32).astype(ml_dtypes.bfloat16).astype(np.float64), axis, -1)
    blocks = v.reshape(v.shape[:-1] + (-1, 32))
    amax = np.abs(blocks).max(-1, keepdims=True)
    byte = np.maximum(np.where(amax > 0, np.frexp(amax)[1] - 1 + 127, 0) - down, 1)
    scale = np.exp2(byte - 127.0)
    codes = (blocks / scale).astype(np.float32).astype(dtype).astype(np.float64)
    return np.moveaxis((codes * scale).reshape(v.shape), -1, axis)


WIDE = False


def mx_kscale(k):
    if not WIDE:
        return np.ones(k)
    levels = np.array([18, -18])
    if k % 512:
        return np.exp2(np.random.permutation(np.resize(levels, k // 32))).repeat(32)
    a = np.empty((k // 512, 16))
    for p in range(k // 512):
        a[p, :8] = np.random.permutation(np.resize(levels, 8))
        for g in range(8):
            far = levels[np.abs(levels - a[p, g]) >= 10]
            a[p, g + 8] = far[np.random.randint(len(far))]
    return np.exp2(a.ravel()).repeat(32)


BF16 = ml_dtypes.bfloat16


def bf(x):
    return np.asarray(x, np.float32).astype(BF16)


def f64(x):
    return np.asarray(x).astype(np.float64)


B, S, H, I = 2, 256, 1024, 2048
T = B * S


def sigmoid(v):
    return 1.0 / (1.0 + np.exp(-v))


def ternary(shape):
    return np.random.randint(-1, 2, shape).astype(np.float64)


def setup_inputs():
    s = mx_kscale(T).reshape(B, S, 1)
    r = mx_kscale(H)
    v = mx_kscale(I)
    x0 = bf(np.random.standard_normal((B, S, H)))
    gate_w0 = bf(ternary((I, H)))
    up_w0 = bf(ternary((I, H)))
    down_w0 = bf(ternary((H, I)))
    gate_s = bf(np.random.uniform(0.5, 2.5, I) / np.sqrt(H))
    up_s = bf(np.random.uniform(0.5, 2.5, I) / np.sqrt(H))
    down_s = bf(np.random.uniform(0.5, 2.5, H) / np.sqrt(I))
    grad_out = bf(4.0 * np.random.standard_normal((B, S, H)) * np.exp2(np.random.randint(-6, 1, (B, S, 1))) / s * r)
    xf = f64(x0).reshape(T, H)
    g = (xf @ f64(gate_w0).T) * f64(gate_s)
    u = (xf @ f64(up_w0).T) * f64(up_s)
    return {"x": bf(f64(x0) * s), "gate_w": bf(f64(gate_w0) / v[:, None]), "up_w": bf(f64(up_w0) / v[:, None]),
            "down_w": bf(f64(down_w0) * v[None, :] / r[:, None]),
            "gate_s": gate_s, "up_s": up_s, "down_s": down_s,
            "g": np.asarray(g, np.float32), "u": np.asarray(u, np.float32), "grad_out": grad_out}


def reference(x, gate_w, up_w, down_w, gate_s, up_s, down_s, g, u, grad_out):
    x = f64(x)
    b, n, h = x.shape
    xf = x.reshape(b * n, h)
    gf, uf = f64(g), f64(u)
    i = gf.shape[1]
    dz2 = f64(grad_out).reshape(b * n, h) * f64(down_s)
    dh = mxq(dz2, 1, "e5m2") @ mxq(f64(down_w), 0, "e4m3")
    sg = sigmoid(gf)
    dg = dh * uf * (sg * (1.0 + gf * (1.0 - sg))) * f64(gate_s)
    du = dh * (gf * sg) * f64(up_s)
    dz1 = np.concatenate([dg, du], axis=1)
    w1 = np.concatenate([f64(gate_w), f64(up_w)], axis=0)
    dx = mxq(dz1, 1, "e5m2") @ mxq(w1, 0, "e4m3")
    dgate_w = mxq(dz1[:, :i], 0, "e5m2").T @ mxq(xf, 0, "e4m3")
    return dx.reshape(b, n, h), dgate_w

@@ -1,0 +1,370 @@
+from contextlib import ExitStack
+
+import concourse.mybir as mybir
+from concourse.masks import make_identity
+
+T, H, I = 512, 1024, 2048
+FLOPS = 2 * T * H * I * 4
+
+F32 = mybir.dt.float32
+BF16 = mybir.dt.bfloat16
+U32 = mybir.dt.uint32
+U8 = mybir.dt.uint8
+E4M3 = mybir.dt.float8_e4m3fn_x4
+E5M2 = mybir.dt.float8_e5m2_x4
+ACT = mybir.ActivationFunctionType
+ALU = mybir.AluOpType
+
+P = 128
+PACK = 4
+W = 512
+GROUPS = I // W
+UNITS = GROUPS * PACK
+DW_LAG = 4
+
+
+def tile_cudaternaryexpertmodule_v_kernel(
+    tc, x, gate_w, up_w, down_w, gate_s, up_s, down_s, g, u, grad_out, out_0, out_1
+):
+    nc = tc.nc
+    go_rows = grad_out.flatten_outer_dims().rearrange("(h p r) c -> h p r c", h=2, r=2)
+    g_rows = g.rearrange("(h p r) c -> h p r c", h=2, r=2)
+    u_rows = u.rearrange("(h p r) c -> h p r c", h=2, r=2)
+    dx_rows = out_0.flatten_outer_dims().rearrange("(h p r) c -> h r p c", h=2, r=2)
+    dw_rows = out_1.rearrange("(q m t) c -> q t m c", t=PACK, m=P)
+    x_rows = x.flatten_outer_dims().rearrange("(p j) c -> p j c", j=PACK)
+    down_rows = down_w.rearrange("(s p j) c -> s p j c", j=PACK, p=P)
+    w1_rows = [w.rearrange("(s p j) c -> s p j c", j=PACK, p=P) for w in (gate_w, up_w)]
+
+    with ExitStack() as ctx:
+        sb = ctx.enter_context(tc.tile_pool(name="sb", bufs=1))
+        ps = ctx.enter_context(tc.psum_pool(name="ps", bufs=1))
+        ctx.enter_context(tc.manual_schedule())
+
+        def sbuf(tag, shape, dtype, bufs):
+            return sb.tile(shape, dtype, name=tag, tag=tag, bufs=bufs, align_bytes=64)
+
+        def bank(b):
+            return ps.tile([P, W], F32, name="bank%d" % b, tag="bank%d" % b)
+
+        tiles = {}
+
+        def load_go(h):
+            tiles["go", h] = sbuf("wide", [P, 2, H], BF16, 8)
+            nc.sync.dma_start(out=tiles["go", h][:], in_=go_rows[h])
+
+        def load_x():
+            tiles["x"] = sbuf("wide", [P, PACK, H], BF16, 8)
+            nc.sync.dma_start(out=tiles["x"][:], in_=x_rows)
+
+        def load_w1(s):
+            tiles["w1", s] = sbuf("wide", [P, PACK, H], BF16, 8)
+            nc.sync.dma_start(out=tiles["w1", s][:], in_=w1_rows[s // GROUPS][s % GROUPS])
+
+        def load_down(q, s):
+            tiles["down", q, s] = sbuf("down", [P, PACK, W], BF16, 3)
+            nc.sync.dma_start(out=tiles["down", q, s][:], in_=down_rows[s][:, :, q * W:(q + 1) * W])
+
+        def load_g(q, h):
+            tiles["g", q, h] = sbuf("g", [P, 2, W], F32, 5)
+            nc.sync.dma_start(out=tiles["g", q, h][:], in_=g_rows[h][:, :, q * W:(q + 1) * W])
+
+        def load_u(q, h):
+            tiles["u", q, h] = sbuf("u", [P, 2, W], F32, 4)
+            nc.sync.dma_start(out=tiles["u", q, h][:], in_=u_rows[h][:, :, q * W:(q + 1) * W])
+
+        def interleave_views(job):
+            dst = tiles["grouped", job][:]
+            if job[0] == "down":
+                src = tiles[job][:]
+                return (dst.rearrange("p (t a b j) -> p a t b j", t=PACK, b=2, j=PACK),
+                        src.rearrange("p j (a b t) -> p a t b j", b=2, t=PACK), 8)
+            if job[0] == "x":
+                src = tiles["x"][:, :, job[1] * W:(job[1] + 1) * W]
+                return (dst.rearrange("p (a i r e) -> p a e r i", i=4, r=2, e=2),
+                        src.rearrange("p (e r) (a i) -> p a e r i", r=2, i=4), 4)
+            if job[0] == "w1":
+                src = tiles["w1", job[1]][:, :, job[2] * W:(job[2] + 1) * W]
+            else:
+                src = tiles[job][:]
+            return (dst.rearrange("p (a i j) -> p a j i", i=4, j=PACK),
+                    src.rearrange("p j (a i) -> p a j i", i=4), 4)
+
+        def start_job(job):
+            tiles["grouped", job] = sbuf("grouped", [P, W * PACK], BF16, 4)
+
+        def interleave_vector(job, cols):
+            dst, src, per = interleave_views(job)
+            nc.vector.tensor_copy(out=dst[:, :cols // per], in_=src[:, :cols // per])
+
+        def interleave_scalar(job, cols):
+            dst, src, per = interleave_views(job)
+            nc.scalar.copy(out=dst[:, cols // per:], in_=src[:, cols // per:])
+
+        def quantize(key, grouped, tag, bufs, fmt):
+            words = grouped.shape[1] // PACK
+            codes = sbuf(tag + "_codes", [P, words], U32, bufs)
+            scales = sbuf(tag + "_scales", [P, words], U8, bufs)
+            nc.vector.quantize_mx(out=codes[:].bitcast(fmt), scales=scales[:], in_=grouped)
+            tiles["mx", key] = (codes, scales, fmt)
+
+        def quantize_job(job):
+            tag, bufs, fmt = {
+                "down": ("weight", 4, E4M3), "w1": ("weight", 4, E4M3), "x": ("x", 2, E4M3),
+                "dg": ("dz1", 8, E5M2), "du": ("dz1", 8, E5M2), "dz2": ("dz2", 2, E5M2),
+            }[job[0]]
+            quantize(job, tiles["grouped", job][:], tag, bufs, fmt)
+
+        def matmul(out, stationary, col0, moving, start, stop):
+            s_codes, s_scales, s_fmt = tiles["mx", stationary]
+            m_codes, m_scales, m_fmt = tiles["mx", moving]
+            nc.tensor.matmul_mx(
+                out=out,
+                lhsT=s_codes[:, col0:col0 + P].bitcast(s_fmt), lhsT_scale=s_scales[:, col0:col0 + P],
+                rhs=m_codes[:].bitcast(m_fmt), rhs_scale=m_scales[:],
+                start=start, stop=stop,
+            )
+
+        def neg_silu(k):
+            q, j = divmod(k, PACK)
+            tiles["n", k] = sbuf("n", [P, W], F32, 2)
+            nc.scalar.activation(out=tiles["n", k][:], in_=tiles["g", q, j % 2][:, j // 2, :], func=ACT.Silu, scale=-1.0)
+
+        def gate_factor(k):
+            q, j = divmod(k, PACK)
+            tiles["f", k] = sbuf("f", [P, PACK, P], F32, 8)
+            nc.vector.scalar_tensor_tensor(
+                out=tiles["f", k][:].rearrange("p t m -> p m t"),
+                in0=tiles["n", k][:].rearrange("p (m t) -> p m t", t=PACK), scalar=1.0,
+                in1=tiles["u", q, j % 2][:, j // 2, :].rearrange("p (m t) -> p m t", t=PACK),
+                op0=ALU.subtract, op1=ALU.mult,
+            )
+
+        def transpose_g(k):
+            q, t = divmod(k, PACK)
+            tiles["gT", k] = bank(k % 2)
+            for j in range(PACK):
+                nc.tensor.transpose(tiles["gT", k][:, j * P:(j + 1) * P],
+                                    tiles["g", q, j % 2][:, j // 2, t:W:PACK], ident[:])
+
+        def transpose_f(k):
+            q, t = divmod(k, PACK)
+            tiles["fT", k] = bank(2)
+            for j in range(PACK):
+                nc.tensor.transpose(tiles["fT", k][:, j * P:(j + 1) * P], tiles["f", q * PACK + j][:, t, :], ident[:])
+
+        def dh_matmul(k):
+            q, t = divmod(k, PACK)
+            tiles["dh", k] = bank(3)
+            for s in range(2):
+                matmul(tiles["dh", k][:], ("down", q, s), t * P, ("dz2", s), s == 0, s == 1)
+
+        def half_tanh(k):
+            tiles["th", k] = sbuf("th", [P, W], F32, 2)
+            nc.scalar.activation(out=tiles["th", k][:], in_=tiles["gT", k][:], func=ACT.Tanh, scale=0.5)
+
+        def sigmoid_dh(k):
+            tiles["e", k] = sbuf("e", [P, W], F32, 2)
+            nc.vector.scalar_tensor_tensor(out=tiles["e", k][:], in0=tiles["th", k][:], scalar=1.0,
+                                           in1=tiles["dh", k][:], op0=ALU.add, op1=ALU.mult)
+
+        def dz1_rows(k):
+            q, t = divmod(k, PACK)
+            if t == 0:
+                tiles["du", q] = sbuf("du", [P, PACK, W], BF16, 2)
+                tiles["dg", q] = sbuf("dg", [P, PACK, W], BF16, 2)
+            for name, factor, other in (("du", up_half, "gT"), ("dg", gate_half, "fT")):
+                nc.vector.scalar_tensor_tensor(out=tiles[name, q][:, t, :], in0=tiles["e", k][:], scalar=factor[:, k:k + 1],
+                                               in1=tiles[other, k][:], op0=ALU.mult, op1=ALU.mult)
+
+        def transpose_dg(k):
+            q, t = divmod(k, PACK)
+            tiles["dgT", k] = bank(4)
+            words = tiles["dg", q][:, t, :].bitcast(F32)
+            for r in range(2):
+                nc.tensor.transpose(tiles["dgT", k][:, r * P:(r + 1) * P], words[:, r * P:(r + 1) * P], ident[:])
+
+        def copy_dg_tokens(k):
+            tiles["dg_tok", k] = sbuf("dg_tok", [P, W], BF16, 2)
+            nc.scalar.copy(out=tiles["dg_tok", k][:].bitcast(F32).rearrange("p (m r) -> p m r", r=2),
+                           in_=tiles["dgT", k][:, :2 * P].rearrange("p (r m) -> p m r", r=2))
+
+        def quantize_dg_tokens(k):
+            quantize(("dg_tok", k), tiles["dg_tok", k][:], "tok", DW_LAG + 1, E5M2)
+
+        def dw_matmul(k):
+            for c in range(2):
+                tiles["dw", k, c] = bank(5 + (2 * k + c) % 3)
+                matmul(tiles["dw", k, c][:], ("dg_tok", k), 0, ("x", c), True, True)
+
+        def dw_store(k):
+            q, t = divmod(k, PACK)
+            result = sbuf("result", [P, 2, W], F32, 3)
+            for c in range(2):
+                nc.scalar.copy(out=result[:, c, :], in_=tiles["dw", k, c][:])
+            nc.sync.dma_start(out=dw_rows[q][t], in_=result[:].rearrange("p c w -> p (c w)"))
+
+        pass_order = [s for q in range(GROUPS) for s in (q, GROUPS + q)]
+
+        def dx_matmul(job):
+            s, c = job[1], job[2]
+            dz1 = ("dg", s) if s < GROUPS else ("du", s - GROUPS)
+            for j in range(PACK):
+                if s == pass_order[0]:
+                    tiles["dx", c, j] = bank(PACK * c + j)
+                matmul(tiles["dx", c, j][:], dz1, j * P, job, s == pass_order[0], s == pass_order[-1])
+
+        def dx_store(c, j, copy):
+            r, h = divmod(j, 2)
+            if r == 0:
+                tiles["dx_out", c, h] = sbuf("result", [P, 2, W], F32, 3)
+            copy(out=tiles["dx_out", c, h][:, r, :], in_=tiles["dx", c, j][:])
+            nc.sync.dma_start(out=dx_rows[h][r][:, c * W:(c + 1) * W], in_=tiles["dx_out", c, h][:, r, :])
+
+        down_scale = sbuf("down_scale", [P, 2, PACK], BF16, 1)
+        gate_scale = sbuf("gate_scale", [P, GROUPS, PACK], BF16, 1)
+        up_scale = sbuf("up_scale", [P, GROUPS, PACK], BF16, 1)
+        nc.scalar.dma_start(out=down_scale[:], in_=down_s.rearrange("(s p t) -> p s t", p=P, t=PACK))
+        load_go(0)
+        load_down(0, 0)
+        load_go(1)
+        load_down(0, 1)
+        load_g(0, 0)
+        load_g(0, 1)
+        load_u(0, 0)
+        load_u(0, 1)
+        nc.sync.dma_start(out=gate_scale[:], in_=gate_s.rearrange("(q p t) -> p q t", p=P, t=PACK))
+        nc.sync.dma_start(out=up_scale[:], in_=up_s.rearrange("(q p t) -> p q t", p=P, t=PACK))
+        load_g(1, 0)
+        load_u(1, 0)
+        load_down(1, 0)
+        load_g(1, 1)
+        load_u(1, 1)
+
+        warm = sbuf("warm", [P, 2], F32, 1)
+        nc.vector.memset(warm[:, 0:1], 0.0)
+        nc.scalar.activation(out=warm[:, 1:2], in_=warm[:, 0:1], func=ACT.Silu)
+        ident = sbuf("ident", [P, P], F32, 1)
+        make_identity(nc, ident[:])
+
+        for s in range(2):
+            start_job(("dz2", s))
+        for h in range(2):
+            words = tiles["go", h][:].bitcast(F32)
+            for s in range(2):
+                turned = bank(4 + 2 * h + s)
+                for d in range(2):
+                    for r in range(2):
+                        nc.tensor.transpose(turned[:, (2 * d + r) * P:(2 * d + r + 1) * P],
+                                            words[:, r, 2 * P * s + d:2 * P * (s + 1):2], ident[:])
+                nc.vector.tensor_tensor(
+                    out=tiles["grouped", ("dz2", s)][:].rearrange("p (r h m d e) -> p h r m d e", r=2, h=2, d=2, e=2)[:, h],
+                    in0=turned[:].bitcast(BF16).rearrange("p (d r m e) -> p r m d e", d=2, r=2, e=2),
+                    in1=down_scale[:, s, :].rearrange("p (d e) -> p d e", e=2).unsqueeze(1).unsqueeze(1).to_broadcast([P, 2, P, 2, 2]),
+                    op=ALU.mult,
+                )
+            start_job(("down", 0, h))
+            interleave_scalar(("down", 0, h), 0)
+        load_down(1, 1)
+        load_x()
+        load_g(2, 0)
+        load_down(2, 0)
+        quantize_job(("down", 0, 0))
+        quantize_job(("dz2", 0))
+        quantize_job(("dz2", 1))
+        quantize_job(("down", 0, 1))
+        gate_half = sbuf("gate_half", [P, UNITS], F32, 1)
+        up_half = sbuf("up_half", [P, UNITS], F32, 1)
+        nc.vector.tensor_scalar(out=gate_half[:], in0=gate_scale[:].rearrange("p q t -> p (q t)"), scalar1=-0.5, scalar2=None, op0=ALU.mult)
+        nc.vector.tensor_scalar(out=up_half[:], in0=up_scale[:].rearrange("p q t -> p (q t)"), scalar1=0.5, scalar2=None, op0=ALU.mult)
+        transpose_g(0)
+        dh_matmul(0)
+        for j in range(PACK):
+            neg_silu(j)
+            if j == 1:
+                half_tanh(0)
+            gate_factor(j)
+        load_u(2, 0)
+        load_u(2, 1)
+
+        jobs = []
+        for q in range(GROUPS):
+            jobs.extend([("down", q + 1, 0), ("down", q + 1, 1)] if q + 1 < GROUPS else [("w1", s, 0) for s in pass_order[:2]])
+            jobs.extend([("dg", q - 1), ("du", q - 1)] if q > 0 else [("x", 0), ("x", 1)])
+        jobs.extend([("w1", pass_order[2], 0), ("dg", GROUPS - 1), ("w1", pass_order[3], 0), ("du", GROUPS - 1)])
+        jobs.extend([("w1", s, 0) for s in pass_order[4:]])
+        jobs.extend([("w1", s, 1) for s in pass_order])
+
+        later_loads = {
+            0: [(load_down, 2, 1), (load_w1, pass_order[0])],
+            1: [(load_down, 3, 0), (load_w1, pass_order[1])],
+            2: [(load_g, 2, 1), (load_g, 3, 0), (load_u, 3, 0)],
+            3: [(load_u, 3, 1), (load_w1, pass_order[2])],
+            4: [(load_down, 3, 1)],
+            5: [(load_w1, pass_order[3])],
+            6: [(load_g, 3, 1)],
+            7: [(load_w1, pass_order[4])],
+            9: [(load_w1, pass_order[5])],
+            11: [(load_w1, pass_order[6])],
+            13: [(load_w1, pass_order[7])],
+        }
+
+        for k in range(UNITS):
+            vector_cols = 128 if k < DW_LAG else 256
+            sigmoid_dh(k)
+            if k > 0:
+                transpose_dg(k - 1)
+            transpose_f(k)
+            if k + PACK < UNITS:
+                neg_silu(k + PACK)
+            if k > 0:
+                copy_dg_tokens(k - 1)
+                quantize_job(jobs[k - 1])
+            if k >= DW_LAG:
+                dw_matmul(k - DW_LAG)
+            dz1_rows(k)
+            if k + 1 < UNITS:
+                transpose_g(k + 1)
+                dh_matmul(k + 1)
+            start_job(jobs[k])
+            interleave_scalar(jobs[k], vector_cols)
+            if k + 1 < UNITS:
+                half_tanh(k + 1)
+            if k >= DW_LAG:
+                dw_store(k - DW_LAG)
+            if k + PACK < UNITS:
+                gate_factor(k + PACK)
+            if k > 0:
+                quantize_dg_tokens(k - 1)
+            interleave_vector(jobs[k], vector_cols)
+            for call in later_loads.get(k, []):
+                call[0](*call[1:])
+
+        transpose_dg(UNITS - 1)
+        copy_dg_tokens(UNITS - 1)
+        for job in jobs[:UNITS]:
+            if job[0] == "w1":
+                dx_matmul(job)
+        first_sweep_end = jobs.index(("w1", pass_order[-1], 0))
+        for k in range(UNITS, len(jobs)):
+            dx_tile = k - first_sweep_end - 2
+            dw_unit = k - DW_LAG
+            vector_cols = 400 if dw_unit < UNITS else 320 if 0 <= dx_tile < PACK else 256
+            start_job(jobs[k])
+            interleave_vector(jobs[k], vector_cols)
+            quantize_job(jobs[k - 1])
+            if k == UNITS:
+                quantize_dg_tokens(UNITS - 1)
+            if dw_unit < UNITS:
+                dw_matmul(dw_unit)
+            if jobs[k - 1][0] == "w1":
+                dx_matmul(jobs[k - 1])
+            interleave_scalar(jobs[k], vector_cols)
+            if dw_unit < UNITS:
+                dw_store(dw_unit)
+            if 0 <= dx_tile < PACK:
+                dx_store(0, dx_tile, nc.scalar.copy)
+        quantize_job(jobs[-1])
+        dx_matmul(jobs[-1])
+        for j in range(PACK):
+            dx_store(1, j, nc.vector.tensor_copy if j % 2 else nc.scalar.copy)

@@ -20,7 +20,11 @@ PACK = 4
 W = 512
 GROUPS = I // W
 UNITS = GROUPS * PACK
-DW_LAG = 4
+DW_LAG = 5
+RB = 4
+X_STEPS = (2, 2, 3, 3)
+W_STEPS = (0, 3, 6, 7, 8, 9, 10, 11)
+SH_A, SH_B, SH_C = 384, 320, 256
 
 
 def tile_cudaternaryexpertmodule_v_kernel(
@@ -75,14 +79,6 @@ def tile_cudaternaryexpertmodule_v_kernel(
 
         def interleave_views(job):
             dst = tiles["grouped", job][:]
-            if job[0] == "down":
-                src = tiles[job][:]
-                return (dst.rearrange("p (t a b j) -> p a t b j", t=PACK, b=2, j=PACK),
-                        src.rearrange("p j (a b t) -> p a t b j", b=2, t=PACK), 8)
-            if job[0] == "x":
-                src = tiles["x"][:, :, job[1] * W:(job[1] + 1) * W]
-                return (dst.rearrange("p (a i r e) -> p a e r i", i=4, r=2, e=2),
-                        src.rearrange("p (e r) (a i) -> p a e r i", r=2, i=4), 4)
             if job[0] == "w1":
                 src = tiles["w1", job[1]][:, :, job[2] * W:(job[2] + 1) * W]
             else:
@@ -108,12 +104,47 @@ def tile_cudaternaryexpertmodule_v_kernel(
             nc.vector.quantize_mx(out=codes[:].bitcast(fmt), scales=scales[:], in_=grouped)
             tiles["mx", key] = (codes, scales, fmt)
 
+        formats = {
+            "down": ("weight", 4, E4M3), "w1": ("weight", 4, E4M3), "x": ("x", 2, E4M3),
+            "dg": ("dz1", 8, E5M2), "du": ("dz1", 8, E5M2), "dz2": ("dz2", 2, E5M2),
+        }
+
         def quantize_job(job):
-            tag, bufs, fmt = {
-                "down": ("weight", 4, E4M3), "w1": ("weight", 4, E4M3), "x": ("x", 2, E4M3),
-                "dg": ("dz1", 8, E5M2), "du": ("dz1", 8, E5M2), "dz2": ("dz2", 2, E5M2),
-            }[job[0]]
+            tag, bufs, fmt = formats[job[0]]
             quantize(job, tiles["grouped", job][:], tag, bufs, fmt)
+
+        def half_views(job, half, dst):
+            cols = slice(half * W // 2, (half + 1) * W // 2)
+            if job[0] == "down":
+                src = tiles[job][:].rearrange("p j (m t) -> p m t j", t=PACK)[:, :, 2 * half:2 * half + 2]
+                return dst.rearrange("p (t m j) -> p m t j", t=2, j=PACK), src
+            if job[0] == "x":
+                src = tiles["x"][:, :, job[1] * W:(job[1] + 1) * W][:, :, cols]
+                return (dst.rearrange("p (a i r e) -> p a e r i", i=4, r=2, e=2),
+                        src.rearrange("p (e r) (a i) -> p a e r i", r=2, i=4))
+            if job[0] == "w1":
+                src = tiles["w1", job[1]][:, :, job[2] * W:(job[2] + 1) * W][:, :, cols]
+            else:
+                src = tiles[job][:, :, cols]
+            return dst.rearrange("p (a i j) -> p a j i", i=4, j=PACK), src.rearrange("p j (a i) -> p a j i", i=4)
+
+        def half_gpsimd(job, half, tag, bufs=1):
+            tiles["grouped", job, half] = sbuf(tag, [P, W * PACK // 2], BF16, bufs)
+            dst, src = half_views(job, half, tiles["grouped", job, half][:])
+            nc.gpsimd.tensor_scalar(out=dst, in0=src, scalar1=1.0, scalar2=0.0, op0=ALU.mult, op1=ALU.add)
+
+        def half_scalar(job, half):
+            tiles["grouped", job, half] = sbuf("grouped", [P, W * PACK // 2], BF16, 4)
+            dst, src = half_views(job, half, tiles["grouped", job, half][:])
+            nc.scalar.copy(out=dst, in_=src)
+
+        def quantize_half(job, half):
+            tag, bufs, fmt = formats[job[0]]
+            if ("mx", job) not in tiles:
+                tiles["mx", job] = (sbuf(tag + "_codes", [P, W], U32, bufs), sbuf(tag + "_scales", [P, W], U8, bufs), fmt)
+            codes, scales, fmt = tiles["mx", job]
+            cols = slice(half * W // 2, (half + 1) * W // 2)
+            nc.vector.quantize_mx(out=codes[:, cols].bitcast(fmt), scales=scales[:, cols], in_=tiles["grouped", job, half][:])
 
         def matmul(out, stationary, col0, moving, start, stop):
             s_codes, s_scales, s_fmt = tiles["mx", stationary]
@@ -127,7 +158,7 @@ def tile_cudaternaryexpertmodule_v_kernel(
 
         def neg_silu(k):
             q, j = divmod(k, PACK)
-            tiles["n", k] = sbuf("n", [P, W], F32, 2)
+            tiles["n", k] = sbuf("n", [P, W], F32, 3)
             nc.scalar.activation(out=tiles["n", k][:], in_=tiles["g", q, j % 2][:, j // 2, :], func=ACT.Silu, scale=-1.0)
 
         def gate_factor(k):
@@ -186,8 +217,8 @@ def tile_cudaternaryexpertmodule_v_kernel(
 
         def copy_dg_tokens(k):
             tiles["dg_tok", k] = sbuf("dg_tok", [P, W], BF16, 2)
-            nc.scalar.copy(out=tiles["dg_tok", k][:].bitcast(F32).rearrange("p (m r) -> p m r", r=2),
-                           in_=tiles["dgT", k][:, :2 * P].rearrange("p (r m) -> p m r", r=2))
+            nc.vector.tensor_copy(out=tiles["dg_tok", k][:].bitcast(F32).rearrange("p (m r) -> p m r", r=2),
+                                  in_=tiles["dgT", k][:, :2 * P].rearrange("p (r m) -> p m r", r=2))
 
         def quantize_dg_tokens(k):
             quantize(("dg_tok", k), tiles["dg_tok", k][:], "tok", DW_LAG + 1, E5M2)
@@ -197,12 +228,13 @@ def tile_cudaternaryexpertmodule_v_kernel(
                 tiles["dw", k, c] = bank(5 + (2 * k + c) % 3)
                 matmul(tiles["dw", k, c][:], ("dg_tok", k), 0, ("x", c), True, True)
 
-        def dw_store(k):
+        def dw_copy(k, c):
             q, t = divmod(k, PACK)
-            result = sbuf("result", [P, 2, W], F32, 3)
-            for c in range(2):
-                nc.scalar.copy(out=result[:, c, :], in_=tiles["dw", k, c][:])
-            nc.sync.dma_start(out=dw_rows[q][t], in_=result[:].rearrange("p c w -> p (c w)"))
+            if c == 0:
+                tiles["dw_out", k] = sbuf("result", [P, 2, W], F32, RB)
+            nc.scalar.copy(out=tiles["dw_out", k][:, c, :], in_=tiles["dw", k, c][:])
+            if c == 1:
+                nc.sync.dma_start(out=dw_rows[q][t], in_=tiles["dw_out", k][:].rearrange("p c w -> p (c w)"))
 
         pass_order = [s for q in range(GROUPS) for s in (q, GROUPS + q)]
 
@@ -217,7 +249,7 @@ def tile_cudaternaryexpertmodule_v_kernel(
         def dx_store(c, j, copy):
             r, h = divmod(j, 2)
             if r == 0:
-                tiles["dx_out", c, h] = sbuf("result", [P, 2, W], F32, 3)
+                tiles["dx_out", c, h] = sbuf("result", [P, 2, W], F32, RB)
             copy(out=tiles["dx_out", c, h][:, r, :], in_=tiles["dx", c, j][:])
             nc.sync.dma_start(out=dx_rows[h][r][:, c * W:(c + 1) * W], in_=tiles["dx_out", c, h][:, r, :])
 
@@ -230,16 +262,14 @@ def tile_cudaternaryexpertmodule_v_kernel(
         load_go(1)
         load_down(0, 1)
         load_g(0, 0)
-        load_g(0, 1)
         load_u(0, 0)
+        load_g(0, 1)
         load_u(0, 1)
         nc.sync.dma_start(out=gate_scale[:], in_=gate_s.rearrange("(q p t) -> p q t", p=P, t=PACK))
         nc.sync.dma_start(out=up_scale[:], in_=up_s.rearrange("(q p t) -> p q t", p=P, t=PACK))
         load_g(1, 0)
-        load_u(1, 0)
         load_down(1, 0)
-        load_g(1, 1)
-        load_u(1, 1)
+        load_u(1, 0)
 
         warm = sbuf("warm", [P, 2], F32, 1)
         nc.vector.memset(warm[:, 0:1], 0.0)
@@ -248,7 +278,7 @@ def tile_cudaternaryexpertmodule_v_kernel(
         make_identity(nc, ident[:])
 
         for s in range(2):
-            start_job(("dz2", s))
+            tiles["grouped", ("dz2", s)] = sbuf("result", [P, W * PACK], BF16, RB)
         for h in range(2):
             words = tiles["go", h][:].bitcast(F32)
             for s in range(2):
@@ -263,105 +293,112 @@ def tile_cudaternaryexpertmodule_v_kernel(
                     in1=down_scale[:, s, :].rearrange("p (d e) -> p d e", e=2).unsqueeze(1).unsqueeze(1).to_broadcast([P, 2, P, 2, 2]),
                     op=ALU.mult,
                 )
-            start_job(("down", 0, h))
-            interleave_scalar(("down", 0, h), 0)
+            half_gpsimd(("down", 0, h), h, *(("gpsimd_grouped", 1) if h else ("grouped", 4)))
+            half_scalar(("down", 0, h), 1 - h)
         load_down(1, 1)
+        load_g(1, 1)
+        load_u(1, 1)
         load_x()
         load_g(2, 0)
         load_down(2, 0)
-        quantize_job(("down", 0, 0))
+        quantize_half(("down", 0, 0), 0)
         quantize_job(("dz2", 0))
+        quantize_half(("down", 0, 1), 0)
         quantize_job(("dz2", 1))
-        quantize_job(("down", 0, 1))
+        dh_matmul(0)
+        transpose_g(0)
+        for j in (0, 2, 1, 3):
+            neg_silu(j)
+            gate_factor(j)
+        half_tanh(0)
         gate_half = sbuf("gate_half", [P, UNITS], F32, 1)
         up_half = sbuf("up_half", [P, UNITS], F32, 1)
         nc.vector.tensor_scalar(out=gate_half[:], in0=gate_scale[:].rearrange("p q t -> p (q t)"), scalar1=-0.5, scalar2=None, op0=ALU.mult)
         nc.vector.tensor_scalar(out=up_half[:], in0=up_scale[:].rearrange("p q t -> p (q t)"), scalar1=0.5, scalar2=None, op0=ALU.mult)
-        transpose_g(0)
-        dh_matmul(0)
-        for j in range(PACK):
-            neg_silu(j)
-            if j == 1:
-                half_tanh(0)
-            gate_factor(j)
+        quantize_half(("down", 0, 0), 1)
+        quantize_half(("down", 0, 1), 1)
         load_u(2, 0)
-        load_u(2, 1)
 
-        jobs = []
-        for q in range(GROUPS):
-            jobs.extend([("down", q + 1, 0), ("down", q + 1, 1)] if q + 1 < GROUPS else [("w1", s, 0) for s in pass_order[:2]])
-            jobs.extend([("dg", q - 1), ("du", q - 1)] if q > 0 else [("x", 0), ("x", 1)])
-        jobs.extend([("w1", pass_order[2], 0), ("dg", GROUPS - 1), ("w1", pass_order[3], 0), ("du", GROUPS - 1)])
+        gpsimd_halves = [(("down", q, s), half) for q in range(1, GROUPS) for half in range(2) for s in range(2)]
+        gpsimd_halves.extend([(("w1", s, 0), half) for s in pass_order[:2] for half in range(2)])
+        x_halves = [(("x", c), half) for c in range(2) for half in range(2)]
+        scalar_halves = [[], [], [], []]
+        scalar_halves.extend([[((name, q), half)] for q in range(GROUPS - 1) for name in ("dg", "du") for half in range(2)])
+        for step, item in zip(X_STEPS, x_halves):
+            scalar_halves[step].append(item)
+        jobs = [("w1", pass_order[2], 0), ("dg", GROUPS - 1), ("w1", pass_order[3], 0), ("du", GROUPS - 1)]
         jobs.extend([("w1", s, 0) for s in pass_order[4:]])
         jobs.extend([("w1", s, 1) for s in pass_order])
 
         later_loads = {
-            0: [(load_down, 2, 1), (load_w1, pass_order[0])],
-            1: [(load_down, 3, 0), (load_w1, pass_order[1])],
-            2: [(load_g, 2, 1), (load_g, 3, 0), (load_u, 3, 0)],
-            3: [(load_u, 3, 1), (load_w1, pass_order[2])],
-            4: [(load_down, 3, 1)],
-            5: [(load_w1, pass_order[3])],
-            6: [(load_g, 3, 1)],
-            7: [(load_w1, pass_order[4])],
-            9: [(load_w1, pass_order[5])],
-            11: [(load_w1, pass_order[6])],
-            13: [(load_w1, pass_order[7])],
+            0: [(load_u, 2, 1)],
+            2: [(load_down, 2, 1), (load_g, 2, 1), (load_g, 3, 0), (load_u, 3, 0)],
+            3: [(load_down, 3, 0), (load_u, 3, 1)],
+            6: [(load_down, 3, 1), (load_g, 3, 1)],
         }
+        for step, s in zip(W_STEPS, pass_order):
+            later_loads.setdefault(step, []).append((load_w1, s))
 
         for k in range(UNITS):
-            vector_cols = 128 if k < DW_LAG else 256
+            ahead = (k // PACK + 1) * PACK + (0, 2, 1, 3)[k % PACK]
+            half_gpsimd(*gpsimd_halves[k], "gpsimd_grouped")
             sigmoid_dh(k)
             if k > 0:
                 transpose_dg(k - 1)
+                copy_dg_tokens(k - 1)
             transpose_f(k)
             if k + PACK < UNITS:
-                neg_silu(k + PACK)
-            if k > 0:
-                copy_dg_tokens(k - 1)
-                quantize_job(jobs[k - 1])
+                neg_silu(ahead)
             if k >= DW_LAG:
                 dw_matmul(k - DW_LAG)
             dz1_rows(k)
             if k + 1 < UNITS:
                 transpose_g(k + 1)
                 dh_matmul(k + 1)
-            start_job(jobs[k])
-            interleave_scalar(jobs[k], vector_cols)
+            if k >= DW_LAG:
+                dw_copy(k - DW_LAG, 0)
             if k + 1 < UNITS:
                 half_tanh(k + 1)
+            for item in scalar_halves[k]:
+                half_scalar(*item)
             if k >= DW_LAG:
-                dw_store(k - DW_LAG)
+                dw_copy(k - DW_LAG, 1)
             if k + PACK < UNITS:
-                gate_factor(k + PACK)
+                gate_factor(ahead)
             if k > 0:
                 quantize_dg_tokens(k - 1)
-            interleave_vector(jobs[k], vector_cols)
+                for item in scalar_halves[k - 1]:
+                    quantize_half(*item)
+            quantize_half(*gpsimd_halves[k])
             for call in later_loads.get(k, []):
                 call[0](*call[1:])
 
         transpose_dg(UNITS - 1)
         copy_dg_tokens(UNITS - 1)
-        for job in jobs[:UNITS]:
-            if job[0] == "w1":
-                dx_matmul(job)
+        quantize_half(*scalar_halves[-1][0])
+        waiting = [("w1", s, 0) for s in pass_order[:2]]
         first_sweep_end = jobs.index(("w1", pass_order[-1], 0))
-        for k in range(UNITS, len(jobs)):
-            dx_tile = k - first_sweep_end - 2
-            dw_unit = k - DW_LAG
-            vector_cols = 400 if dw_unit < UNITS else 320 if 0 <= dx_tile < PACK else 256
-            start_job(jobs[k])
-            interleave_vector(jobs[k], vector_cols)
-            quantize_job(jobs[k - 1])
-            if k == UNITS:
+        for i, job in enumerate(jobs):
+            dx_tile = i - first_sweep_end - 2
+            dw_unit = UNITS + i - DW_LAG
+            vector_cols = SH_A if dw_unit < UNITS or i + 1 == len(jobs) else SH_B if 0 <= dx_tile < PACK else SH_C
+            start_job(job)
+            interleave_vector(job, vector_cols)
+            if i == 0:
                 quantize_dg_tokens(UNITS - 1)
+            else:
+                quantize_job(jobs[i - 1])
             if dw_unit < UNITS:
                 dw_matmul(dw_unit)
-            if jobs[k - 1][0] == "w1":
-                dx_matmul(jobs[k - 1])
-            interleave_scalar(jobs[k], vector_cols)
+            if i > 0 and jobs[i - 1][0] == "w1":
+                waiting.append(jobs[i - 1])
+            for ready in waiting[:1 if dw_unit < UNITS else 2]:
+                dx_matmul(ready)
+                waiting.remove(ready)
+            interleave_scalar(job, vector_cols)
             if dw_unit < UNITS:
-                dw_store(dw_unit)
+                dw_copy(dw_unit, 0)
+                dw_copy(dw_unit, 1)
             if 0 <= dx_tile < PACK:
                 dx_store(0, dx_tile, nc.scalar.copy)
         quantize_job(jobs[-1])

from contextlib import ExitStack

import concourse.mybir as mybir
from concourse.masks import make_identity

T, H, I = 512, 1024, 2048
FLOPS = 2 * T * H * I * 4

F32 = mybir.dt.float32
BF16 = mybir.dt.bfloat16
U32 = mybir.dt.uint32
U8 = mybir.dt.uint8
E4M3 = mybir.dt.float8_e4m3fn_x4
E5M2 = mybir.dt.float8_e5m2_x4
ACT = mybir.ActivationFunctionType
ALU = mybir.AluOpType

P = 128
PACK = 4
W = 512
GROUPS = I // W
UNITS = GROUPS * PACK
DW_LAG = 5
RB = 4
X_STEPS = (2, 2, 3, 3)
W_STEPS = (0, 3, 6, 7, 8, 9, 10, 11)
SH_A, SH_B, SH_C = 384, 320, 256


def tile_cudaternaryexpertmodule_v_kernel(
    tc, x, gate_w, up_w, down_w, gate_s, up_s, down_s, g, u, grad_out, out_0, out_1
):
    nc = tc.nc
    go_rows = grad_out.flatten_outer_dims().rearrange("(h p r) c -> h p r c", h=2, r=2)
    g_rows = g.rearrange("(h p r) c -> h p r c", h=2, r=2)
    u_rows = u.rearrange("(h p r) c -> h p r c", h=2, r=2)
    dx_rows = out_0.flatten_outer_dims().rearrange("(h p r) c -> h r p c", h=2, r=2)
    dw_rows = out_1.rearrange("(q m t) c -> q t m c", t=PACK, m=P)
    x_rows = x.flatten_outer_dims().rearrange("(p j) c -> p j c", j=PACK)
    down_rows = down_w.rearrange("(s p j) c -> s p j c", j=PACK, p=P)
    w1_rows = [w.rearrange("(s p j) c -> s p j c", j=PACK, p=P) for w in (gate_w, up_w)]

    with ExitStack() as ctx:
        sb = ctx.enter_context(tc.tile_pool(name="sb", bufs=1))
        ps = ctx.enter_context(tc.psum_pool(name="ps", bufs=1))
        ctx.enter_context(tc.manual_schedule())

        def sbuf(tag, shape, dtype, bufs):
            return sb.tile(shape, dtype, name=tag, tag=tag, bufs=bufs, align_bytes=64)

        def bank(b):
            return ps.tile([P, W], F32, name="bank%d" % b, tag="bank%d" % b)

        tiles = {}

        def load_go(h):
            tiles["go", h] = sbuf("wide", [P, 2, H], BF16, 8)
            nc.sync.dma_start(out=tiles["go", h][:], in_=go_rows[h])

        def load_x():
            tiles["x"] = sbuf("wide", [P, PACK, H], BF16, 8)
            nc.sync.dma_start(out=tiles["x"][:], in_=x_rows)

        def load_w1(s):
            tiles["w1", s] = sbuf("wide", [P, PACK, H], BF16, 8)
            nc.sync.dma_start(out=tiles["w1", s][:], in_=w1_rows[s // GROUPS][s % GROUPS])

        def load_down(q, s):
            tiles["down", q, s] = sbuf("down", [P, PACK, W], BF16, 3)
            nc.sync.dma_start(out=tiles["down", q, s][:], in_=down_rows[s][:, :, q * W:(q + 1) * W])

        def load_g(q, h):
            tiles["g", q, h] = sbuf("g", [P, 2, W], F32, 5)
            nc.sync.dma_start(out=tiles["g", q, h][:], in_=g_rows[h][:, :, q * W:(q + 1) * W])

        def load_u(q, h):
            tiles["u", q, h] = sbuf("u", [P, 2, W], F32, 4)
            nc.sync.dma_start(out=tiles["u", q, h][:], in_=u_rows[h][:, :, q * W:(q + 1) * W])

        def interleave_views(job):
            dst = tiles["grouped", job][:]
            if job[0] == "w1":
                src = tiles["w1", job[1]][:, :, job[2] * W:(job[2] + 1) * W]
            else:
                src = tiles[job][:]
            return (dst.rearrange("p (a i j) -> p a j i", i=4, j=PACK),
                    src.rearrange("p j (a i) -> p a j i", i=4), 4)

        def start_job(job):
            tiles["grouped", job] = sbuf("grouped", [P, W * PACK], BF16, 4)

        def interleave_vector(job, cols):
            dst, src, per = interleave_views(job)
            nc.vector.tensor_copy(out=dst[:, :cols // per], in_=src[:, :cols // per])

        def interleave_scalar(job, cols):
            dst, src, per = interleave_views(job)
            nc.scalar.copy(out=dst[:, cols // per:], in_=src[:, cols // per:])

        def quantize(key, grouped, tag, bufs, fmt):
            words = grouped.shape[1] // PACK
            codes = sbuf(tag + "_codes", [P, words], U32, bufs)
            scales = sbuf(tag + "_scales", [P, words], U8, bufs)
            nc.vector.quantize_mx(out=codes[:].bitcast(fmt), scales=scales[:], in_=grouped)
            tiles["mx", key] = (codes, scales, fmt)

        formats = {
            "down": ("weight", 4, E4M3), "w1": ("weight", 4, E4M3), "x": ("x", 2, E4M3),
            "dg": ("dz1", 8, E5M2), "du": ("dz1", 8, E5M2), "dz2": ("dz2", 2, E5M2),
        }

        def quantize_job(job):
            tag, bufs, fmt = formats[job[0]]
            quantize(job, tiles["grouped", job][:], tag, bufs, fmt)

        def half_views(job, half, dst):
            cols = slice(half * W // 2, (half + 1) * W // 2)
            if job[0] == "down":
                src = tiles[job][:].rearrange("p j (m t) -> p m t j", t=PACK)[:, :, 2 * half:2 * half + 2]
                return dst.rearrange("p (t m j) -> p m t j", t=2, j=PACK), src
            if job[0] == "x":
                src = tiles["x"][:, :, job[1] * W:(job[1] + 1) * W][:, :, cols]
                return (dst.rearrange("p (a i r e) -> p a e r i", i=4, r=2, e=2),
                        src.rearrange("p (e r) (a i) -> p a e r i", r=2, i=4))
            if job[0] == "w1":
                src = tiles["w1", job[1]][:, :, job[2] * W:(job[2] + 1) * W][:, :, cols]
            else:
                src = tiles[job][:, :, cols]
            return dst.rearrange("p (a i j) -> p a j i", i=4, j=PACK), src.rearrange("p j (a i) -> p a j i", i=4)

        def half_gpsimd(job, half, tag, bufs=1):
            tiles["grouped", job, half] = sbuf(tag, [P, W * PACK // 2], BF16, bufs)
            dst, src = half_views(job, half, tiles["grouped", job, half][:])
            nc.gpsimd.tensor_scalar(out=dst, in0=src, scalar1=1.0, scalar2=0.0, op0=ALU.mult, op1=ALU.add)

        def half_scalar(job, half):
            tiles["grouped", job, half] = sbuf("grouped", [P, W * PACK // 2], BF16, 4)
            dst, src = half_views(job, half, tiles["grouped", job, half][:])
            nc.scalar.copy(out=dst, in_=src)

        def quantize_half(job, half):
            tag, bufs, fmt = formats[job[0]]
            if ("mx", job) not in tiles:
                tiles["mx", job] = (sbuf(tag + "_codes", [P, W], U32, bufs), sbuf(tag + "_scales", [P, W], U8, bufs), fmt)
            codes, scales, fmt = tiles["mx", job]
            cols = slice(half * W // 2, (half + 1) * W // 2)
            nc.vector.quantize_mx(out=codes[:, cols].bitcast(fmt), scales=scales[:, cols], in_=tiles["grouped", job, half][:])

        def matmul(out, stationary, col0, moving, start, stop):
            s_codes, s_scales, s_fmt = tiles["mx", stationary]
            m_codes, m_scales, m_fmt = tiles["mx", moving]
            nc.tensor.matmul_mx(
                out=out,
                lhsT=s_codes[:, col0:col0 + P].bitcast(s_fmt), lhsT_scale=s_scales[:, col0:col0 + P],
                rhs=m_codes[:].bitcast(m_fmt), rhs_scale=m_scales[:],
                start=start, stop=stop,
            )

        def neg_silu(k):
            q, j = divmod(k, PACK)
            tiles["n", k] = sbuf("n", [P, W], F32, 3)
            nc.scalar.activation(out=tiles["n", k][:], in_=tiles["g", q, j % 2][:, j // 2, :], func=ACT.Silu, scale=-1.0)

        def gate_factor(k):
            q, j = divmod(k, PACK)
            tiles["f", k] = sbuf("f", [P, PACK, P], F32, 8)
            nc.vector.scalar_tensor_tensor(
                out=tiles["f", k][:].rearrange("p t m -> p m t"),
                in0=tiles["n", k][:].rearrange("p (m t) -> p m t", t=PACK), scalar=1.0,
                in1=tiles["u", q, j % 2][:, j // 2, :].rearrange("p (m t) -> p m t", t=PACK),
                op0=ALU.subtract, op1=ALU.mult,
            )

        def transpose_g(k):
            q, t = divmod(k, PACK)
            tiles["gT", k] = bank(k % 2)
            for j in range(PACK):
                nc.tensor.transpose(tiles["gT", k][:, j * P:(j + 1) * P],
                                    tiles["g", q, j % 2][:, j // 2, t:W:PACK], ident[:])

        def transpose_f(k):
            q, t = divmod(k, PACK)
            tiles["fT", k] = bank(2)
            for j in range(PACK):
                nc.tensor.transpose(tiles["fT", k][:, j * P:(j + 1) * P], tiles["f", q * PACK + j][:, t, :], ident[:])

        def dh_matmul(k):
            q, t = divmod(k, PACK)
            tiles["dh", k] = bank(3)
            for s in range(2):
                matmul(tiles["dh", k][:], ("down", q, s), t * P, ("dz2", s), s == 0, s == 1)

        def half_tanh(k):
            tiles["th", k] = sbuf("th", [P, W], F32, 2)
            nc.scalar.activation(out=tiles["th", k][:], in_=tiles["gT", k][:], func=ACT.Tanh, scale=0.5)

        def sigmoid_dh(k):
            tiles["e", k] = sbuf("e", [P, W], F32, 2)
            nc.vector.scalar_tensor_tensor(out=tiles["e", k][:], in0=tiles["th", k][:], scalar=1.0,
                                           in1=tiles["dh", k][:], op0=ALU.add, op1=ALU.mult)

        def dz1_rows(k):
            q, t = divmod(k, PACK)
            if t == 0:
                tiles["du", q] = sbuf("du", [P, PACK, W], BF16, 2)
                tiles["dg", q] = sbuf("dg", [P, PACK, W], BF16, 2)
            for name, factor, other in (("du", up_half, "gT"), ("dg", gate_half, "fT")):
                nc.vector.scalar_tensor_tensor(out=tiles[name, q][:, t, :], in0=tiles["e", k][:], scalar=factor[:, k:k + 1],
                                               in1=tiles[other, k][:], op0=ALU.mult, op1=ALU.mult)

        def transpose_dg(k):
            q, t = divmod(k, PACK)
            tiles["dgT", k] = bank(4)
            words = tiles["dg", q][:, t, :].bitcast(F32)
            for r in range(2):
                nc.tensor.transpose(tiles["dgT", k][:, r * P:(r + 1) * P], words[:, r * P:(r + 1) * P], ident[:])

        def copy_dg_tokens(k):
            tiles["dg_tok", k] = sbuf("dg_tok", [P, W], BF16, 2)
            nc.vector.tensor_copy(out=tiles["dg_tok", k][:].bitcast(F32).rearrange("p (m r) -> p m r", r=2),
                                  in_=tiles["dgT", k][:, :2 * P].rearrange("p (r m) -> p m r", r=2))

        def quantize_dg_tokens(k):
            quantize(("dg_tok", k), tiles["dg_tok", k][:], "tok", DW_LAG + 1, E5M2)

        def dw_matmul(k):
            for c in range(2):
                tiles["dw", k, c] = bank(5 + (2 * k + c) % 3)
                matmul(tiles["dw", k, c][:], ("dg_tok", k), 0, ("x", c), True, True)

        def dw_copy(k, c):
            q, t = divmod(k, PACK)
            if c == 0:
                tiles["dw_out", k] = sbuf("result", [P, 2, W], F32, RB)
            nc.scalar.copy(out=tiles["dw_out", k][:, c, :], in_=tiles["dw", k, c][:])
            if c == 1:
                nc.sync.dma_start(out=dw_rows[q][t], in_=tiles["dw_out", k][:].rearrange("p c w -> p (c w)"))

        pass_order = [s for q in range(GROUPS) for s in (q, GROUPS + q)]

        def dx_matmul(job):
            s, c = job[1], job[2]
            dz1 = ("dg", s) if s < GROUPS else ("du", s - GROUPS)
            for j in range(PACK):
                if s == pass_order[0]:
                    tiles["dx", c, j] = bank(PACK * c + j)
                matmul(tiles["dx", c, j][:], dz1, j * P, job, s == pass_order[0], s == pass_order[-1])

        def dx_store(c, j, copy):
            r, h = divmod(j, 2)
            if r == 0:
                tiles["dx_out", c, h] = sbuf("result", [P, 2, W], F32, RB)
            copy(out=tiles["dx_out", c, h][:, r, :], in_=tiles["dx", c, j][:])
            nc.sync.dma_start(out=dx_rows[h][r][:, c * W:(c + 1) * W], in_=tiles["dx_out", c, h][:, r, :])

        down_scale = sbuf("down_scale", [P, 2, PACK], BF16, 1)
        gate_scale = sbuf("gate_scale", [P, GROUPS, PACK], BF16, 1)
        up_scale = sbuf("up_scale", [P, GROUPS, PACK], BF16, 1)
        nc.scalar.dma_start(out=down_scale[:], in_=down_s.rearrange("(s p t) -> p s t", p=P, t=PACK))
        load_go(0)
        load_down(0, 0)
        load_go(1)
        load_down(0, 1)
        load_g(0, 0)
        load_u(0, 0)
        load_g(0, 1)
        load_u(0, 1)
        nc.sync.dma_start(out=gate_scale[:], in_=gate_s.rearrange("(q p t) -> p q t", p=P, t=PACK))
        nc.sync.dma_start(out=up_scale[:], in_=up_s.rearrange("(q p t) -> p q t", p=P, t=PACK))
        load_g(1, 0)
        load_down(1, 0)
        load_u(1, 0)

        warm = sbuf("warm", [P, 2], F32, 1)
        nc.vector.memset(warm[:, 0:1], 0.0)
        nc.scalar.activation(out=warm[:, 1:2], in_=warm[:, 0:1], func=ACT.Silu)
        ident = sbuf("ident", [P, P], F32, 1)
        make_identity(nc, ident[:])

        for s in range(2):
            tiles["grouped", ("dz2", s)] = sbuf("result", [P, W * PACK], BF16, RB)
        for h in range(2):
            words = tiles["go", h][:].bitcast(F32)
            for s in range(2):
                turned = bank(4 + 2 * h + s)
                for d in range(2):
                    for r in range(2):
                        nc.tensor.transpose(turned[:, (2 * d + r) * P:(2 * d + r + 1) * P],
                                            words[:, r, 2 * P * s + d:2 * P * (s + 1):2], ident[:])
                nc.vector.tensor_tensor(
                    out=tiles["grouped", ("dz2", s)][:].rearrange("p (r h m d e) -> p h r m d e", r=2, h=2, d=2, e=2)[:, h],
                    in0=turned[:].bitcast(BF16).rearrange("p (d r m e) -> p r m d e", d=2, r=2, e=2),
                    in1=down_scale[:, s, :].rearrange("p (d e) -> p d e", e=2).unsqueeze(1).unsqueeze(1).to_broadcast([P, 2, P, 2, 2]),
                    op=ALU.mult,
                )
            half_gpsimd(("down", 0, h), h, *(("gpsimd_grouped", 1) if h else ("grouped", 4)))
            half_scalar(("down", 0, h), 1 - h)
        load_down(1, 1)
        load_g(1, 1)
        load_u(1, 1)
        load_x()
        load_g(2, 0)
        load_down(2, 0)
        quantize_half(("down", 0, 0), 0)
        quantize_job(("dz2", 0))
        quantize_half(("down", 0, 1), 0)
        quantize_job(("dz2", 1))
        dh_matmul(0)
        transpose_g(0)
        for j in (0, 2, 1, 3):
            neg_silu(j)
            gate_factor(j)
        half_tanh(0)
        gate_half = sbuf("gate_half", [P, UNITS], F32, 1)
        up_half = sbuf("up_half", [P, UNITS], F32, 1)
        nc.vector.tensor_scalar(out=gate_half[:], in0=gate_scale[:].rearrange("p q t -> p (q t)"), scalar1=-0.5, scalar2=None, op0=ALU.mult)
        nc.vector.tensor_scalar(out=up_half[:], in0=up_scale[:].rearrange("p q t -> p (q t)"), scalar1=0.5, scalar2=None, op0=ALU.mult)
        quantize_half(("down", 0, 0), 1)
        quantize_half(("down", 0, 1), 1)
        load_u(2, 0)

        gpsimd_halves = [(("down", q, s), half) for q in range(1, GROUPS) for half in range(2) for s in range(2)]
        gpsimd_halves.extend([(("w1", s, 0), half) for s in pass_order[:2] for half in range(2)])
        x_halves = [(("x", c), half) for c in range(2) for half in range(2)]
        scalar_halves = [[], [], [], []]
        scalar_halves.extend([[((name, q), half)] for q in range(GROUPS - 1) for name in ("dg", "du") for half in range(2)])
        for step, item in zip(X_STEPS, x_halves):
            scalar_halves[step].append(item)
        jobs = [("w1", pass_order[2], 0), ("dg", GROUPS - 1), ("w1", pass_order[3], 0), ("du", GROUPS - 1)]
        jobs.extend([("w1", s, 0) for s in pass_order[4:]])
        jobs.extend([("w1", s, 1) for s in pass_order])

        later_loads = {
            0: [(load_u, 2, 1)],
            2: [(load_down, 2, 1), (load_g, 2, 1), (load_g, 3, 0), (load_u, 3, 0)],
            3: [(load_down, 3, 0), (load_u, 3, 1)],
            6: [(load_down, 3, 1), (load_g, 3, 1)],
        }
        for step, s in zip(W_STEPS, pass_order):
            later_loads.setdefault(step, []).append((load_w1, s))

        for k in range(UNITS):
            ahead = (k // PACK + 1) * PACK + (0, 2, 1, 3)[k % PACK]
            half_gpsimd(*gpsimd_halves[k], "gpsimd_grouped")
            sigmoid_dh(k)
            if k > 0:
                transpose_dg(k - 1)
                copy_dg_tokens(k - 1)
            transpose_f(k)
            if k + PACK < UNITS:
                neg_silu(ahead)
            if k >= DW_LAG:
                dw_matmul(k - DW_LAG)
            dz1_rows(k)
            if k + 1 < UNITS:
                transpose_g(k + 1)
                dh_matmul(k + 1)
            if k >= DW_LAG:
                dw_copy(k - DW_LAG, 0)
            if k + 1 < UNITS:
                half_tanh(k + 1)
            for item in scalar_halves[k]:
                half_scalar(*item)
            if k >= DW_LAG:
                dw_copy(k - DW_LAG, 1)
            if k + PACK < UNITS:
                gate_factor(ahead)
            if k > 0:
                quantize_dg_tokens(k - 1)
                for item in scalar_halves[k - 1]:
                    quantize_half(*item)
            quantize_half(*gpsimd_halves[k])
            for call in later_loads.get(k, []):
                call[0](*call[1:])

        transpose_dg(UNITS - 1)
        copy_dg_tokens(UNITS - 1)
        quantize_half(*scalar_halves[-1][0])
        waiting = [("w1", s, 0) for s in pass_order[:2]]
        first_sweep_end = jobs.index(("w1", pass_order[-1], 0))
        for i, job in enumerate(jobs):
            dx_tile = i - first_sweep_end - 2
            dw_unit = UNITS + i - DW_LAG
            vector_cols = SH_A if dw_unit < UNITS or i + 1 == len(jobs) else SH_B if 0 <= dx_tile < PACK else SH_C
            start_job(job)
            interleave_vector(job, vector_cols)
            if i == 0:
                quantize_dg_tokens(UNITS - 1)
            else:
                quantize_job(jobs[i - 1])
            if dw_unit < UNITS:
                dw_matmul(dw_unit)
            if i > 0 and jobs[i - 1][0] == "w1":
                waiting.append(jobs[i - 1])
            for ready in waiting[:1 if dw_unit < UNITS else 2]:
                dx_matmul(ready)
                waiting.remove(ready)
            interleave_scalar(job, vector_cols)
            if dw_unit < UNITS:
                dw_copy(dw_unit, 0)
                dw_copy(dw_unit, 1)
            if 0 <= dx_tile < PACK:
                dx_store(0, dx_tile, nc.scalar.copy)
        quantize_job(jobs[-1])
        dx_matmul(jobs[-1])
        for j in range(PACK):
            dx_store(1, j, nc.vector.tensor_copy if j % 2 else nc.scalar.copy)
